import numpy as np
import ml_dtypes

BF16 = ml_dtypes.bfloat16


def bf(x):
    return np.asarray(x, np.float32).astype(BF16)


def f32(x):
    return np.asarray(x, np.float32)


def f64(x):
    return np.asarray(x).astype(np.float64)


def striped(idx):
    return np.tile(idx.reshape(-1, 16).T, (8, 1))


S, D, R, N = 2048, 128, 4, 8192
EPS = 1e-8


def setup_inputs():
    dist = 2.0 * np.random.random_sample((R, S))
    wts = np.exp(-dist)
    wts = wts / (wts.sum(axis=0, keepdims=True) + EPS)
    return {"x": bf(np.random.standard_normal((S, D))), "w_in": bf(np.random.standard_normal((D, D)) / np.sqrt(D)), "w_out": bf(np.random.standard_normal((D, D)) / np.sqrt(D)), "b_out": f32(0.1 * np.random.standard_normal((D, 1))), "fw": f32(wts.reshape(1, N)), "offs": striped(np.concatenate([np.random.permutation(S) for _ in range(R)]))}


def reference(x, w_in, w_out, b_out, fw, offs):
    idx = offs[:16].T.reshape(-1)
    h = f64(w_in).T @ f64(x)[idx].T
    fused = (h * f64(fw)).reshape(D, R, S).sum(axis=1)
    return f64(x).T + f64(w_out).T @ fused + f64(b_out)

@@ -1,0 +1,79 @@
+import concourse.masks as masks
+import concourse.mybir as mybir
+
+BF16, F32, U16 = mybir.dt.bfloat16, mybir.dt.float32, mybir.dt.uint16
+MULT, ADD = mybir.AluOpType.mult, mybir.AluOpType.add
+
+P = 128
+S = 2048
+R = 4
+N = R * S
+PIECE = 512
+CHUNKS = S // PIECE
+BLOCKS = PIECE // P
+
+FLOPS = 2 * P * P * N + 2 * P * P * S
+
+
+def tile_cantormultiheadfusion_kernel(tc, x, w_in, w_out, b_out, fw, offs, out):
+    nc = tc.nc
+    fw_row = fw.rearrange("o n -> (o n)")
+    with (
+        tc.tile_pool(name="held", bufs=1) as held,
+        tc.tile_pool(name="work", bufs=3) as work,
+        tc.psum_pool(name="banks", bufs=6) as banks,
+        tc.psum_pool(name="t_banks", bufs=2) as t_banks,
+    ):
+        offsets = held.tile([P, N // 16], U16, name="offsets")
+        nc.sync.dma_start(offsets[:], offs)
+        identity = held.tile([P, P], BF16, name="identity")
+        masks.make_identity(nc, identity[:])
+        x_blocks = x.rearrange("(n p) d -> p n d", p=P)
+        table = held.tile([P, S], BF16, name="table")
+        for c in range(CHUNKS):
+            rows = held.tile([P, BLOCKS, P], BF16, name=f"rows{c}")
+            nc.scalar.dma_start(rows[:], x_blocks[:, c * BLOCKS : (c + 1) * BLOCKS, :])
+            flipped = t_banks.tile([P, PIECE], BF16, name="flipped")
+            for b in range(BLOCKS):
+                nc.tensor.transpose(flipped[:, b * P : (b + 1) * P], rows[:, b, :], identity[:])
+            nc.vector.tensor_copy(table[:, c * PIECE : (c + 1) * PIECE], flipped[:])
+        w_in_sb = held.tile([P, P], BF16, name="w_in_sb")
+        nc.sync.dma_start(w_in_sb[:], w_in)
+        w_out_sb = held.tile([P, P], BF16, name="w_out_sb")
+        nc.sync.dma_start(w_out_sb[:], w_out)
+        bias = held.tile([P, 1], F32, name="bias")
+        nc.sync.dma_start(bias[:], b_out)
+
+        weights = held.tile([P, N], F32, name="weights")
+        for c in range(CHUNKS):
+            for r in range(R):
+                j = r * S + c * PIECE
+                nc.sync.dma_start(weights[:, j : j + PIECE], fw_row[j : j + PIECE].partition_broadcast(P))
+
+        fused = []
+        for c in range(CHUNKS):
+            total = None
+            for r in range(R):
+                j = r * S + c * PIECE
+                h = banks.tile([P, PIECE], F32, name="h", tag="bank")
+                nc.tensor.matmul(
+                    h[:], w_in_sb[:], table[:].indirect(offsets[:, j // 16 : (j + PIECE) // 16]),
+                    start=True, stop=True,
+                )
+                product = work.tile([P, PIECE], F32, name="product")
+                nc.vector.tensor_tensor(product[:], h[:], weights[:, j : j + PIECE], MULT)
+                if r == 0:
+                    total = product
+                else:
+                    summed = work.tile([P, PIECE], BF16 if r == R - 1 else F32, name=f"summed{r}", bufs=CHUNKS)
+                    nc.vector.tensor_tensor(summed[:], total[:], product[:], ADD)
+                    total = summed
+            fused.append(total)
+        for c in range(CHUNKS):
+            projected = banks.tile([P, PIECE], F32, name="projected", tag="bank")
+            nc.tensor.matmul(projected[:], w_out_sb[:], fused[c][:], start=True, stop=True)
+            result = work.tile([P, PIECE], F32, name="result")
+            nc.vector.scalar_tensor_tensor(
+                result[:], projected[:], bias[:, 0:1], table[:, c * PIECE : (c + 1) * PIECE], ADD, ADD
+            )
+            nc.sync.dma_start(out[:, c * PIECE : (c + 1) * PIECE], result[:])

@@ -3,6 +3,7 @@ import concourse.mybir as mybir
 
 BF16, F32, U16 = mybir.dt.bfloat16, mybir.dt.float32, mybir.dt.uint16
 MULT, ADD = mybir.AluOpType.mult, mybir.AluOpType.add
+IDENTITY = mybir.ActivationFunctionType.Identity
 
 P = 128
 S = 2048
@@ -20,7 +21,7 @@ def tile_cantormultiheadfusion_kernel(tc, x, w_in, w_out, b_out, fw, offs, out):
     fw_row = fw.rearrange("o n -> (o n)")
     with (
         tc.tile_pool(name="held", bufs=1) as held,
-        tc.tile_pool(name="work", bufs=3) as work,
+        tc.tile_pool(name="work", bufs=4) as work,
         tc.psum_pool(name="banks", bufs=6) as banks,
         tc.psum_pool(name="t_banks", bufs=2) as t_banks,
     ):
@@ -64,16 +65,19 @@ def tile_cantormultiheadfusion_kernel(tc, x, w_in, w_out, b_out, fw, offs, out):
                 nc.vector.tensor_tensor(product[:], h[:], weights[:, j : j + PIECE], MULT)
                 if r == 0:
                     total = product
+                elif r < R - 1:
+                    summed = work.tile([P, PIECE], F32, name=f"summed{r}")
+                    nc.gpsimd.tensor_tensor(summed[:], total[:], product[:], ADD)
+                    total = summed
                 else:
-                    summed = work.tile([P, PIECE], BF16 if r == R - 1 else F32, name=f"summed{r}", bufs=CHUNKS)
+                    summed = work.tile([P, PIECE], BF16, name="fused", bufs=CHUNKS)
                     nc.vector.tensor_tensor(summed[:], total[:], product[:], ADD)
                     total = summed
             fused.append(total)
         for c in range(CHUNKS):
             projected = banks.tile([P, PIECE], F32, name="projected", tag="bank")
-            nc.tensor.matmul(projected[:], w_out_sb[:], fused[c][:], start=True, stop=True)
+            nc.tensor.matmul(projected[:], w_out_sb[:], fused[c][:], start=True, stop=False)
+            nc.tensor.matmul(projected[:], identity[:], table[:, c * PIECE : (c + 1) * PIECE], start=False, stop=True)
             result = work.tile([P, PIECE], F32, name="result")
-            nc.vector.scalar_tensor_tensor(
-                result[:], projected[:], bias[:, 0:1], table[:, c * PIECE : (c + 1) * PIECE], ADD, ADD
-            )
+            nc.scalar.activation(result[:], projected[:], IDENTITY, bias=bias[:, 0:1])
             nc.sync.dma_start(out[:, c * PIECE : (c + 1) * PIECE], result[:])

@@ -11,6 +11,7 @@ R = 4
 N = R * S
 PIECE = 512
 CHUNKS = S // PIECE
+LAG = 2
 BLOCKS = PIECE // P
 
 FLOPS = 2 * P * P * N + 2 * P * P * S
@@ -21,40 +22,46 @@ def tile_cantormultiheadfusion_kernel(tc, x, w_in, w_out, b_out, fw, offs, out):
     fw_row = fw.rearrange("o n -> (o n)")
     with (
         tc.tile_pool(name="held", bufs=1) as held,
-        tc.tile_pool(name="work", bufs=4) as work,
+        tc.tile_pool(name="work", bufs=6) as work,
         tc.psum_pool(name="banks", bufs=6) as banks,
         tc.psum_pool(name="t_banks", bufs=2) as t_banks,
     ):
+        x_chunks = x.rearrange("(c p b) d -> p c (b d)", p=P, b=BLOCKS)
+        rows = held.tile([P, CHUNKS, BLOCKS * P], BF16, name="rows")
+        for c in range(CHUNKS):
+            queue = nc.sync if c % 2 == 0 else nc.scalar
+            queue.dma_start(rows[:, c, :], x_chunks[:, c, :])
         offsets = held.tile([P, N // 16], U16, name="offsets")
         nc.sync.dma_start(offsets[:], offs)
-        identity = held.tile([P, P], BF16, name="identity")
-        masks.make_identity(nc, identity[:])
-        x_blocks = x.rearrange("(n p) d -> p n d", p=P)
-        table = held.tile([P, S], BF16, name="table")
-        for c in range(CHUNKS):
-            rows = held.tile([P, BLOCKS, P], BF16, name=f"rows{c}")
-            nc.scalar.dma_start(rows[:], x_blocks[:, c * BLOCKS : (c + 1) * BLOCKS, :])
-            flipped = t_banks.tile([P, PIECE], BF16, name="flipped")
-            for b in range(BLOCKS):
-                nc.tensor.transpose(flipped[:, b * P : (b + 1) * P], rows[:, b, :], identity[:])
-            nc.vector.tensor_copy(table[:, c * PIECE : (c + 1) * PIECE], flipped[:])
         w_in_sb = held.tile([P, P], BF16, name="w_in_sb")
         nc.sync.dma_start(w_in_sb[:], w_in)
+        weights = held.tile([P, N], F32, name="weights")
+        for k in range(N // PIECE):
+            c, r = divmod(k, R)
+            j = r * S + c * PIECE
+            nc.sync.dma_start(weights[:, j : j + PIECE], fw_row[j : j + PIECE].partition_broadcast(P))
         w_out_sb = held.tile([P, P], BF16, name="w_out_sb")
         nc.sync.dma_start(w_out_sb[:], w_out)
         bias = held.tile([P, 1], F32, name="bias")
         nc.sync.dma_start(bias[:], b_out)
 
-        weights = held.tile([P, N], F32, name="weights")
+        identity = held.tile([P, P], BF16, name="identity")
+        masks.make_identity(nc, identity[:])
+        table = held.tile([P, S], BF16, name="table")
         for c in range(CHUNKS):
-            for r in range(R):
-                j = r * S + c * PIECE
-                nc.sync.dma_start(weights[:, j : j + PIECE], fw_row[j : j + PIECE].partition_broadcast(P))
+            flipped = t_banks.tile([P, BLOCKS, P], BF16, name="flipped")
+            for b in range(BLOCKS):
+                nc.tensor.transpose(flipped[:, b, :], rows[:, c, b * P : (b + 1) * P], identity[:])
+            copy = nc.vector.tensor_copy if c % 2 == 0 else nc.scalar.copy
+            copy(
+                table[:, c * PIECE : (c + 1) * PIECE].rearrange("d (p b) -> d p b", b=BLOCKS),
+                flipped[:].rearrange("d b p -> d p b"),
+            )
 
-        fused = []
-        for c in range(CHUNKS):
-            total = None
-            for r in range(R):
+        inner, last, fused = {}, {}, {}
+        for k in range(N // PIECE + LAG):
+            if k < N // PIECE:
+                c, r = divmod(k, R)
                 j = r * S + c * PIECE
                 h = banks.tile([P, PIECE], F32, name="h", tag="bank")
                 nc.tensor.matmul(
@@ -64,20 +71,25 @@ def tile_cantormultiheadfusion_kernel(tc, x, w_in, w_out, b_out, fw, offs, out):
                 product = work.tile([P, PIECE], F32, name="product")
                 nc.vector.tensor_tensor(product[:], h[:], weights[:, j : j + PIECE], MULT)
                 if r == 0:
-                    total = product
+                    inner[c] = product
                 elif r < R - 1:
-                    summed = work.tile([P, PIECE], F32, name=f"summed{r}")
-                    nc.gpsimd.tensor_tensor(summed[:], total[:], product[:], ADD)
-                    total = summed
+                    summed = work.tile([P, PIECE], F32, name="summed")
+                    nc.gpsimd.tensor_tensor(summed[:], inner[c][:], product[:], ADD)
+                    inner[c] = summed
                 else:
-                    summed = work.tile([P, PIECE], BF16, name="fused", bufs=CHUNKS)
-                    nc.vector.tensor_tensor(summed[:], total[:], product[:], ADD)
-                    total = summed
-            fused.append(total)
+                    last[c] = product
+            if k >= LAG and (k - LAG) % R == R - 1:
+                c = (k - LAG) // R
+                fused[c] = held.tile([P, PIECE], BF16, name=f"fused{c}")
+                nc.vector.tensor_tensor(fused[c][:], inner[c][:], last[c][:], ADD)
+        projected = {}
         for c in range(CHUNKS):
-            projected = banks.tile([P, PIECE], F32, name="projected", tag="bank")
-            nc.tensor.matmul(projected[:], w_out_sb[:], fused[c][:], start=True, stop=False)
-            nc.tensor.matmul(projected[:], identity[:], table[:, c * PIECE : (c + 1) * PIECE], start=False, stop=True)
+            projected[c] = banks.tile([P, PIECE], F32, name="projected", tag="bank")
+            nc.tensor.matmul(
+                projected[c][:], identity[:], table[:, c * PIECE : (c + 1) * PIECE], start=True, stop=False
+            )
+        for c in range(CHUNKS):
+            nc.tensor.matmul(projected[c][:], w_out_sb[:], fused[c][:], start=False, stop=True)
             result = work.tile([P, PIECE], F32, name="result")
-            nc.scalar.activation(result[:], projected[:], IDENTITY, bias=bias[:, 0:1])
+            nc.scalar.activation(result[:], projected[c][:], IDENTITY, bias=bias[:, 0:1])
             nc.sync.dma_start(out[:, c * PIECE : (c + 1) * PIECE], result[:])

@@ -11,7 +11,6 @@ R = 4
 N = R * S
 PIECE = 512
 CHUNKS = S // PIECE
-LAG = 2
 BLOCKS = PIECE // P
 
 FLOPS = 2 * P * P * N + 2 * P * P * S
@@ -20,9 +19,10 @@ FLOPS = 2 * P * P * N + 2 * P * P * S
 def tile_cantormultiheadfusion_kernel(tc, x, w_in, w_out, b_out, fw, offs, out):
     nc = tc.nc
     fw_row = fw.rearrange("o n -> (o n)")
+    pieces = [(r, c) for c in range(CHUNKS) for r in (0, 1)] + [(r, c) for r in (2, 3) for c in range(CHUNKS)]
     with (
         tc.tile_pool(name="held", bufs=1) as held,
-        tc.tile_pool(name="work", bufs=6) as work,
+        tc.tile_pool(name="work", bufs=8) as work,
         tc.psum_pool(name="banks", bufs=6) as banks,
         tc.psum_pool(name="t_banks", bufs=2) as t_banks,
     ):
@@ -34,12 +34,14 @@ def tile_cantormultiheadfusion_kernel(tc, x, w_in, w_out, b_out, fw, offs, out):
         offsets = held.tile([P, N // 16], U16, name="offsets")
         nc.sync.dma_start(offsets[:], offs)
         w_in_sb = held.tile([P, P], BF16, name="w_in_sb")
-        nc.sync.dma_start(w_in_sb[:], w_in)
+        nc.scalar.dma_start(w_in_sb[:], w_in)
         weights = held.tile([P, N], F32, name="weights")
-        for k in range(N // PIECE):
-            c, r = divmod(k, R)
-            j = r * S + c * PIECE
-            nc.sync.dma_start(weights[:, j : j + PIECE], fw_row[j : j + PIECE].partition_broadcast(P))
+        for r, c in pieces:
+            if c % 2 == 0:
+                j = r * S + c * PIECE
+                nc.sync.dma_start(
+                    weights[:, j : j + 2 * PIECE], fw_row[j : j + 2 * PIECE].partition_broadcast(P)
+                )
         w_out_sb = held.tile([P, P], BF16, name="w_out_sb")
         nc.sync.dma_start(w_out_sb[:], w_out)
         bias = held.tile([P, 1], F32, name="bias")
@@ -58,30 +60,25 @@ def tile_cantormultiheadfusion_kernel(tc, x, w_in, w_out, b_out, fw, offs, out):
                 flipped[:].rearrange("d b p -> d p b"),
             )
 
-        inner, last, fused = {}, {}, {}
-        for k in range(N // PIECE + LAG):
-            if k < N // PIECE:
-                c, r = divmod(k, R)
-                j = r * S + c * PIECE
-                h = banks.tile([P, PIECE], F32, name="h", tag="bank")
-                nc.tensor.matmul(
-                    h[:], w_in_sb[:], table[:].indirect(offsets[:, j // 16 : (j + PIECE) // 16]),
-                    start=True, stop=True,
-                )
-                product = work.tile([P, PIECE], F32, name="product")
-                nc.vector.tensor_tensor(product[:], h[:], weights[:, j : j + PIECE], MULT)
-                if r == 0:
-                    inner[c] = product
-                elif r < R - 1:
-                    summed = work.tile([P, PIECE], F32, name="summed")
-                    nc.gpsimd.tensor_tensor(summed[:], inner[c][:], product[:], ADD)
-                    inner[c] = summed
-                else:
-                    last[c] = product
-            if k >= LAG and (k - LAG) % R == R - 1:
-                c = (k - LAG) // R
+        total, fused = {}, {}
+        for r, c in pieces:
+            j = r * S + c * PIECE
+            h = banks.tile([P, PIECE], F32, name="h", tag="bank")
+            nc.tensor.matmul(
+                h[:], w_in_sb[:], table[:].indirect(offsets[:, j // 16 : (j + PIECE) // 16]),
+                start=True, stop=True,
+            )
+            product = work.tile([P, PIECE], F32, name="product")
+            nc.vector.tensor_tensor(product[:], h[:], weights[:, j : j + PIECE], MULT)
+            if r == 0:
+                total[c] = product
+            elif r < R - 1:
+                summed = work.tile([P, PIECE], F32, name="summed")
+                nc.gpsimd.tensor_tensor(summed[:], total[c][:], product[:], ADD)
+                total[c] = summed
+            else:
                 fused[c] = held.tile([P, PIECE], BF16, name=f"fused{c}")
-                nc.vector.tensor_tensor(fused[c][:], inner[c][:], last[c][:], ADD)
+                nc.vector.tensor_tensor(fused[c][:], total[c][:], product[:], ADD)
         projected = {}
         for c in range(CHUNKS):
             projected[c] = banks.tile([P, PIECE], F32, name="projected", tag="bank")

@@ -73,8 +73,9 @@ def tile_cantormultiheadfusion_kernel(tc, x, w_in, w_out, b_out, fw, offs, out):
             if r == 0:
                 total[c] = product
             elif r < R - 1:
+                adder = nc.vector if (r, c) == (2, 0) else nc.gpsimd
                 summed = work.tile([P, PIECE], F32, name="summed")
-                nc.gpsimd.tensor_tensor(summed[:], total[c][:], product[:], ADD)
+                adder.tensor_tensor(summed[:], total[c][:], product[:], ADD)
                 total[c] = summed
             else:
                 fused[c] = held.tile([P, PIECE], BF16, name=f"fused{c}")

@@ -54,8 +54,7 @@ def tile_cantormultiheadfusion_kernel(tc, x, w_in, w_out, b_out, fw, offs, out):
             flipped = t_banks.tile([P, BLOCKS, P], BF16, name="flipped")
             for b in range(BLOCKS):
                 nc.tensor.transpose(flipped[:, b, :], rows[:, c, b * P : (b + 1) * P], identity[:])
-            copy = nc.vector.tensor_copy if c % 2 == 0 else nc.scalar.copy
-            copy(
+            nc.vector.tensor_copy(
                 table[:, c * PIECE : (c + 1) * PIECE].rearrange("d (p b) -> d p b", b=BLOCKS),
                 flipped[:].rearrange("d b p -> d p b"),
             )

@@ -19,7 +19,7 @@ FLOPS = 2 * P * P * N + 2 * P * P * S
 def tile_cantormultiheadfusion_kernel(tc, x, w_in, w_out, b_out, fw, offs, out):
     nc = tc.nc
     fw_row = fw.rearrange("o n -> (o n)")
-    pieces = [(r, c) for c in range(CHUNKS) for r in (0, 1)] + [(r, c) for r in (2, 3) for c in range(CHUNKS)]
+    pieces = [(r, c) for r in range(R) for c in range(CHUNKS)]
     with (
         tc.tile_pool(name="held", bufs=1) as held,
         tc.tile_pool(name="work", bufs=8) as work,
@@ -36,12 +36,8 @@ def tile_cantormultiheadfusion_kernel(tc, x, w_in, w_out, b_out, fw, offs, out):
         w_in_sb = held.tile([P, P], BF16, name="w_in_sb")
         nc.scalar.dma_start(w_in_sb[:], w_in)
         weights = held.tile([P, N], F32, name="weights")
-        for r, c in pieces:
-            if c % 2 == 0:
-                j = r * S + c * PIECE
-                nc.sync.dma_start(
-                    weights[:, j : j + 2 * PIECE], fw_row[j : j + 2 * PIECE].partition_broadcast(P)
-                )
+        for r in range(R):
+            nc.sync.dma_start(weights[:, r * S : (r + 1) * S], fw_row[r * S : (r + 1) * S].partition_broadcast(P))
         w_out_sb = held.tile([P, P], BF16, name="w_out_sb")
         nc.sync.dma_start(w_out_sb[:], w_out)
         bias = held.tile([P, 1], F32, name="bias")

@@ -23,14 +23,12 @@ def tile_cantormultiheadfusion_kernel(tc, x, w_in, w_out, b_out, fw, offs, out):
     with (
         tc.tile_pool(name="held", bufs=1) as held,
         tc.tile_pool(name="work", bufs=8) as work,
-        tc.psum_pool(name="banks", bufs=6) as banks,
-        tc.psum_pool(name="t_banks", bufs=2) as t_banks,
+        tc.psum_pool(name="banks", bufs=8) as banks,
     ):
         x_chunks = x.rearrange("(c p b) d -> p c (b d)", p=P, b=BLOCKS)
         rows = held.tile([P, CHUNKS, BLOCKS * P], BF16, name="rows")
-        for c in range(CHUNKS):
-            queue = nc.sync if c % 2 == 0 else nc.scalar
-            queue.dma_start(rows[:, c, :], x_chunks[:, c, :])
+        for c in range(0, CHUNKS, 2):
+            nc.sync.dma_start(rows[:, c : c + 2, :], x_chunks[:, c : c + 2, :])
         offsets = held.tile([P, N // 16], U16, name="offsets")
         nc.sync.dma_start(offsets[:], offs)
         w_in_sb = held.tile([P, P], BF16, name="w_in_sb")
@@ -47,7 +45,7 @@ def tile_cantormultiheadfusion_kernel(tc, x, w_in, w_out, b_out, fw, offs, out):
         masks.make_identity(nc, identity[:])
         table = held.tile([P, S], BF16, name="table")
         for c in range(CHUNKS):
-            flipped = t_banks.tile([P, BLOCKS, P], BF16, name="flipped")
+            flipped = banks.tile([P, BLOCKS, P], BF16, name="flipped", tag="bank")
             for b in range(BLOCKS):
                 nc.tensor.transpose(flipped[:, b, :], rows[:, c, b * P : (b + 1) * P], identity[:])
             nc.vector.tensor_copy(
@@ -68,7 +66,7 @@ def tile_cantormultiheadfusion_kernel(tc, x, w_in, w_out, b_out, fw, offs, out):
             if r == 0:
                 total[c] = product
             elif r < R - 1:
-                adder = nc.vector if (r, c) == (2, 0) else nc.gpsimd
+                adder = nc.vector if (r, c) in ((1, CHUNKS - 1), (2, 0)) else nc.gpsimd
                 summed = work.tile([P, PIECE], F32, name="summed")
                 adder.tensor_tensor(summed[:], total[c][:], product[:], ADD)
                 total[c] = summed

@@ -27,8 +27,9 @@ def tile_cantormultiheadfusion_kernel(tc, x, w_in, w_out, b_out, fw, offs, out):
     ):
         x_chunks = x.rearrange("(c p b) d -> p c (b d)", p=P, b=BLOCKS)
         rows = held.tile([P, CHUNKS, BLOCKS * P], BF16, name="rows")
-        for c in range(0, CHUNKS, 2):
-            nc.sync.dma_start(rows[:, c : c + 2, :], x_chunks[:, c : c + 2, :])
+        for c in range(CHUNKS):
+            queue = nc.sync if c % 2 == 0 else nc.scalar
+            queue.dma_start(rows[:, c, :], x_chunks[:, c, :])
         offsets = held.tile([P, N // 16], U16, name="offsets")
         nc.sync.dma_start(offsets[:], offs)
         w_in_sb = held.tile([P, P], BF16, name="w_in_sb")

@@ -84,4 +84,5 @@ def tile_cantormultiheadfusion_kernel(tc, x, w_in, w_out, b_out, fw, offs, out):
             nc.tensor.matmul(projected[c][:], w_out_sb[:], fused[c][:], start=False, stop=True)
             result = work.tile([P, PIECE], F32, name="result")
             nc.scalar.activation(result[:], projected[c][:], IDENTITY, bias=bias[:, 0:1])
-            nc.sync.dma_start(out[:, c * PIECE : (c + 1) * PIECE], result[:])
+            queue = nc.scalar if c == CHUNKS - 1 else nc.sync
+            queue.dma_start(out[:, c * PIECE : (c + 1) * PIECE], result[:])

import concourse.masks as masks
import concourse.mybir as mybir

BF16, F32, U16 = mybir.dt.bfloat16, mybir.dt.float32, mybir.dt.uint16
MULT, ADD = mybir.AluOpType.mult, mybir.AluOpType.add
IDENTITY = mybir.ActivationFunctionType.Identity

P = 128
S = 2048
R = 4
N = R * S
PIECE = 512
CHUNKS = S // PIECE
BLOCKS = PIECE // P

FLOPS = 2 * P * P * N + 2 * P * P * S


def tile_cantormultiheadfusion_kernel(tc, x, w_in, w_out, b_out, fw, offs, out):
    nc = tc.nc
    fw_row = fw.rearrange("o n -> (o n)")
    pieces = [(r, c) for r in range(R) for c in range(CHUNKS)]
    with (
        tc.tile_pool(name="held", bufs=1) as held,
        tc.tile_pool(name="work", bufs=8) as work,
        tc.psum_pool(name="banks", bufs=8) as banks,
    ):
        x_chunks = x.rearrange("(c p b) d -> p c (b d)", p=P, b=BLOCKS)
        rows = held.tile([P, CHUNKS, BLOCKS * P], BF16, name="rows")
        for c in range(CHUNKS):
            queue = nc.sync if c % 2 == 0 else nc.scalar
            queue.dma_start(rows[:, c, :], x_chunks[:, c, :])
        offsets = held.tile([P, N // 16], U16, name="offsets")
        nc.sync.dma_start(offsets[:], offs)
        w_in_sb = held.tile([P, P], BF16, name="w_in_sb")
        nc.scalar.dma_start(w_in_sb[:], w_in)
        weights = held.tile([P, N], F32, name="weights")
        for r in range(R):
            nc.sync.dma_start(weights[:, r * S : (r + 1) * S], fw_row[r * S : (r + 1) * S].partition_broadcast(P))
        w_out_sb = held.tile([P, P], BF16, name="w_out_sb")
        nc.sync.dma_start(w_out_sb[:], w_out)
        bias = held.tile([P, 1], F32, name="bias")
        nc.sync.dma_start(bias[:], b_out)

        identity = held.tile([P, P], BF16, name="identity")
        masks.make_identity(nc, identity[:])
        table = held.tile([P, S], BF16, name="table")
        for c in range(CHUNKS):
            flipped = banks.tile([P, BLOCKS, P], BF16, name="flipped", tag="bank")
            for b in range(BLOCKS):
                nc.tensor.transpose(flipped[:, b, :], rows[:, c, b * P : (b + 1) * P], identity[:])
            nc.vector.tensor_copy(
                table[:, c * PIECE : (c + 1) * PIECE].rearrange("d (p b) -> d p b", b=BLOCKS),
                flipped[:].rearrange("d b p -> d p b"),
            )

        total, fused = {}, {}
        for r, c in pieces:
            j = r * S + c * PIECE
            h = banks.tile([P, PIECE], F32, name="h", tag="bank")
            nc.tensor.matmul(
                h[:], w_in_sb[:], table[:].indirect(offsets[:, j // 16 : (j + PIECE) // 16]),
                start=True, stop=True,
            )
            product = work.tile([P, PIECE], F32, name="product")
            nc.vector.tensor_tensor(product[:], h[:], weights[:, j : j + PIECE], MULT)
            if r == 0:
                total[c] = product
            elif r < R - 1:
                adder = nc.vector if (r, c) in ((1, CHUNKS - 1), (2, 0)) else nc.gpsimd
                summed = work.tile([P, PIECE], F32, name="summed")
                adder.tensor_tensor(summed[:], total[c][:], product[:], ADD)
                total[c] = summed
            else:
                fused[c] = held.tile([P, PIECE], BF16, name=f"fused{c}")
                nc.vector.tensor_tensor(fused[c][:], total[c][:], product[:], ADD)
        projected = {}
        for c in range(CHUNKS):
            projected[c] = banks.tile([P, PIECE], F32, name="projected", tag="bank")
            nc.tensor.matmul(
                projected[c][:], identity[:], table[:, c * PIECE : (c + 1) * PIECE], start=True, stop=False
            )
        for c in range(CHUNKS):
            nc.tensor.matmul(projected[c][:], w_out_sb[:], fused[c][:], start=False, stop=True)
            result = work.tile([P, PIECE], F32, name="result")
            nc.scalar.activation(result[:], projected[c][:], IDENTITY, bias=bias[:, 0:1])
            queue = nc.scalar if c == CHUNKS - 1 else nc.sync
            queue.dma_start(out[:, c * PIECE : (c + 1) * PIECE], result[:])
